import numpy as np
import ml_dtypes


def mxq(x, axis, fmt="e4m3"):
    dtype, down = {"e4m3": (ml_dtypes.float8_e4m3fn, 7), "e5m2": (ml_dtypes.float8_e5m2, 14)}[fmt]
    v = np.moveaxis(np.asarray(x, np.float32).astype(ml_dtypes.bfloat16).astype(np.float64), axis, -1)
    blocks = v.reshape(v.shape[:-1] + (-1, 32))
    amax = np.abs(blocks).max(-1, keepdims=True)
    byte = np.maximum(np.where(amax > 0, np.frexp(amax)[1] - 1 + 127, 0) - down, 1)
    scale = np.exp2(byte - 127.0)
    codes = (blocks / scale).astype(np.float32).astype(dtype).astype(np.float64)
    return np.moveaxis((codes * scale).reshape(v.shape), -1, axis)


BF16 = ml_dtypes.bfloat16


def bf(x):
    return np.asarray(x, np.float32).astype(BF16)


def f64(x):
    return np.asarray(x).astype(np.float64)


B, C, N, H, W = 64, 1, 16384, 64, 64

SIGMA0 = 2.0


def setup_inputs():
    return {"batch_images": bf(np.random.standard_normal((B, C, H, W))),
            "batch_labels": bf(np.random.random_sample((B, N, 2)) * np.array([W, H])),
            "sigma": bf(SIGMA0 * (1.0 + 0.1 * np.random.standard_normal(1)))}


def reference(batch_images, batch_labels, sigma):
    img = f64(batch_images)
    lab = f64(batch_labels)
    sg = f64(sigma)
    Hh = img.shape[2]
    Ww = img.shape[3]
    xs = np.arange(Ww, dtype=np.float64)
    ys = np.arange(Hh, dtype=np.float64)
    lx = lab[..., 0]
    ly = lab[..., 1]
    inv = 1.0 / (2.0 * sg * sg)
    gx = np.exp(-((xs[None, None, :] - lx[..., None]) ** 2) * inv)
    gy = np.exp(-((ys[None, None, :] - ly[..., None]) ** 2) * inv)
    gx = gx / np.sum(gx, axis=-1, keepdims=True)
    gy = gy / np.sum(gy, axis=-1, keepdims=True)
    density = mxq(gy, 1, "e4m3").transpose(0, 2, 1) @ mxq(gx, 1, "e4m3")
    return density[:, None, :, :]

@@ -1,0 +1,130 @@
+from contextlib import ExitStack
+
+import concourse.mybir as mybir
+
+F32 = mybir.dt.float32
+BF16 = mybir.dt.bfloat16
+U32 = mybir.dt.uint32
+U8 = mybir.dt.uint8
+FP8X4 = mybir.dt.float8_e4m3fn_x4
+ACT = mybir.ActivationFunctionType
+ALU = mybir.AluOpType
+
+P = 128
+PACK = 4
+K_PASS = P * PACK
+XY = 2
+QUANT_WIDTH = 4096
+CHUNK_PASSES = 16
+STORE_IMAGES = 8
+
+IMAGES, LABELS, PIXELS = 64, 16384, 64
+FLOPS = 2 * IMAGES * LABELS * PIXELS * PIXELS
+BYTES = IMAGES * LABELS * XY * 2 + 2 + IMAGES * PIXELS * PIXELS * 4
+
+
+def tile_dmg_k_kernel(tc, batch_images, batch_labels, sigma, out):
+    nc = tc.nc
+    images, labels = batch_labels.shape[0], batch_labels.shape[1]
+    height, width = out.shape[2], out.shape[3]
+    assert height == width and XY * width == P
+    pixels = width
+    passes = labels // K_PASS
+    assert labels % K_PASS == 0 and passes % CHUNK_PASSES == 0 and images % STORE_IMAGES == 0
+    chunks = passes // CHUNK_PASSES
+    slots = XY * CHUNK_PASSES
+    chunk_values = slots * pixels * PACK
+    assert chunk_values % QUANT_WIDTH == 0
+
+    with ExitStack() as ctx:
+        const = ctx.enter_context(tc.tile_pool(name="const", bufs=1))
+        label_pool = ctx.enter_context(tc.tile_pool(name="labels", bufs=3))
+        gauss_pool = ctx.enter_context(tc.tile_pool(name="gauss", bufs=3))
+        sum_pool = ctx.enter_context(tc.tile_pool(name="sums", bufs=3))
+        norm_pool = ctx.enter_context(tc.tile_pool(name="norm", bufs=2))
+        mx_pool = ctx.enter_context(tc.tile_pool(name="mx", bufs=3))
+        map_pool = ctx.enter_context(tc.tile_pool(name="maps", bufs=2))
+        psum = ctx.enter_context(tc.psum_pool(name="psum", bufs=2))
+
+        sigma_bf = const.tile([P, 1], BF16)
+        nc.sync.dma_start(out=sigma_bf[:], in_=sigma.partition_broadcast(P))
+        sigma_f = const.tile([P, 1], F32)
+        nc.vector.tensor_copy(out=sigma_f[:], in_=sigma_bf[:])
+        minus_two_var = const.tile([P, 1], F32)
+        nc.vector.scalar_tensor_tensor(
+            out=minus_two_var[:], in0=sigma_f[:], scalar=-2.0, in1=sigma_f[:], op0=ALU.mult, op1=ALU.mult
+        )
+        minus_inv = const.tile([P, 1], F32)
+        nc.vector.reciprocal(out=minus_inv[:], in_=minus_two_var[:])
+
+        for b in range(images):
+            lab = label_pool.tile([P, passes, PACK * XY], BF16)
+            nc.sync.dma_start(
+                out=lab[:], in_=batch_labels[b].rearrange("(g p j) t -> p g (j t)", p=P, j=PACK)
+            )
+            if b % STORE_IMAGES == 0:
+                maps = map_pool.tile([P, STORE_IMAGES, pixels], F32)
+            acc = psum.tile([P, P], F32)
+
+            for k in range(chunks):
+                chunk_lab = lab[:, k * CHUNK_PASSES : (k + 1) * CHUNK_PASSES, :].rearrange(
+                    "p g (j t) -> p g t j", t=XY
+                )
+                gauss = gauss_pool.tile([P, pixels, slots, PACK], F32)
+                for c in range(pixels):
+                    nc.scalar.activation(
+                        out=gauss[:, c].rearrange("p (g t) j -> p g t j", t=XY),
+                        in_=chunk_lab,
+                        func=ACT.Square,
+                        bias=float(-c),
+                    )
+                whole = gauss[:].rearrange("p c s j -> p (c s j)")
+                nc.scalar.activation(out=whole, in_=whole, func=ACT.Exp, scale=minus_inv[:, 0:1])
+
+                sums = sum_pool.tile([P, slots, PACK], F32)
+                nc.vector.tensor_reduce(
+                    out=sums[:],
+                    in_=gauss[:].rearrange("p c s j -> p s j c"),
+                    axis=mybir.AxisListType.X,
+                    op=ALU.add,
+                )
+                recip = sum_pool.tile([P, slots, PACK], F32)
+                nc.vector.reciprocal(out=recip[:], in_=sums[:])
+
+                grouped = norm_pool.tile([P, slots, pixels, PACK], BF16, align_bytes=64)
+                nc.vector.tensor_tensor(
+                    out=grouped[:],
+                    in0=gauss[:].rearrange("p c s j -> p s c j"),
+                    in1=recip[:].unsqueeze(2).to_broadcast([P, slots, pixels, PACK]),
+                    op=ALU.mult,
+                )
+
+                codes = mx_pool.tile([P, slots * pixels], U32, align_bytes=64)
+                scales = mx_pool.tile([P, slots * pixels], U8, align_bytes=64)
+                flat = grouped[:].rearrange("p s c j -> p (s c j)")
+                for q in range(chunk_values // QUANT_WIDTH):
+                    words = slice(q * QUANT_WIDTH // PACK, (q + 1) * QUANT_WIDTH // PACK)
+                    nc.vector.quantize_mx(
+                        out=codes[:, words].bitcast(FP8X4),
+                        scales=scales[:, words],
+                        in_=flat[:, q * QUANT_WIDTH : (q + 1) * QUANT_WIDTH],
+                    )
+
+                for g in range(CHUNK_PASSES):
+                    cols = slice(g * P, (g + 1) * P)
+                    nc.tensor.matmul_mx(
+                        out=acc[:],
+                        lhsT=codes[:, cols].bitcast(FP8X4),
+                        lhsT_scale=scales[:, cols],
+                        rhs=codes[:, cols].bitcast(FP8X4),
+                        rhs_scale=scales[:, cols],
+                        start=(k == 0 and g == 0),
+                        stop=(k == chunks - 1 and g == CHUNK_PASSES - 1),
+                    )
+
+            nc.scalar.copy(out=maps[pixels:P, b % STORE_IMAGES, :], in_=acc[pixels:P, 0:pixels])
+            if b % STORE_IMAGES == STORE_IMAGES - 1:
+                first = b - (STORE_IMAGES - 1)
+                nc.sync.dma_start(
+                    out=out[first : b + 1, 0].rearrange("b h w -> h b w"), in_=maps[pixels:P, :, :]
+                )

@@ -40,6 +40,7 @@ def tile_dmg_k_kernel(tc, batch_images, batch_labels, sigma, out):
         const = ctx.enter_context(tc.tile_pool(name="const", bufs=1))
         label_pool = ctx.enter_context(tc.tile_pool(name="labels", bufs=3))
         gauss_pool = ctx.enter_context(tc.tile_pool(name="gauss", bufs=3))
+        fold_pool = ctx.enter_context(tc.tile_pool(name="fold", bufs=2))
         sum_pool = ctx.enter_context(tc.tile_pool(name="sums", bufs=3))
         norm_pool = ctx.enter_context(tc.tile_pool(name="norm", bufs=2))
         mx_pool = ctx.enter_context(tc.tile_pool(name="mx", bufs=3))
@@ -81,15 +82,18 @@ def tile_dmg_k_kernel(tc, batch_images, batch_labels, sigma, out):
                 whole = gauss[:].rearrange("p c s j -> p (c s j)")
                 nc.scalar.activation(out=whole, in_=whole, func=ACT.Exp, scale=minus_inv[:, 0:1])
 
-                sums = sum_pool.tile([P, slots, PACK], F32)
-                nc.vector.tensor_reduce(
-                    out=sums[:],
-                    in_=gauss[:].rearrange("p c s j -> p s j c"),
-                    axis=mybir.AxisListType.X,
-                    op=ALU.add,
+                folded = fold_pool.tile([P, pixels // 2, slots, PACK], F32)
+                nc.vector.tensor_tensor(
+                    out=folded[:], in0=gauss[:, 0 : pixels // 2], in1=gauss[:, pixels // 2 : pixels], op=ALU.add
                 )
+                left = pixels // 4
+                while left >= 1:
+                    nc.vector.tensor_tensor(
+                        out=folded[:, 0:left], in0=folded[:, 0:left], in1=folded[:, left : 2 * left], op=ALU.add
+                    )
+                    left //= 2
                 recip = sum_pool.tile([P, slots, PACK], F32)
-                nc.vector.reciprocal(out=recip[:], in_=sums[:])
+                nc.vector.reciprocal(out=recip[:], in_=folded[:, 0])
 
                 grouped = norm_pool.tile([P, slots, pixels, PACK], BF16, align_bytes=64)
                 nc.vector.tensor_tensor(

@@ -1,6 +1,7 @@
 from contextlib import ExitStack
 
 import concourse.mybir as mybir
+from concourse.masks import make_identity
 
 F32 = mybir.dt.float32
 BF16 = mybir.dt.bfloat16
@@ -17,6 +18,7 @@ XY = 2
 QUANT_WIDTH = 4096
 CHUNK_PASSES = 16
 STORE_IMAGES = 8
+POOL_FOLDS = 2
 
 IMAGES, LABELS, PIXELS = 64, 16384, 64
 FLOPS = 2 * IMAGES * LABELS * PIXELS * PIXELS
@@ -46,6 +48,10 @@ def tile_dmg_k_kernel(tc, batch_images, batch_labels, sigma, out):
         mx_pool = ctx.enter_context(tc.tile_pool(name="mx", bufs=3))
         map_pool = ctx.enter_context(tc.tile_pool(name="maps", bufs=2))
         psum = ctx.enter_context(tc.psum_pool(name="psum", bufs=2))
+        recip_psum = ctx.enter_context(tc.psum_pool(name="recip_psum", bufs=2))
+
+        ident = const.tile([P, P], F32)
+        make_identity(nc, ident[:])
 
         sigma_bf = const.tile([P, 1], BF16)
         nc.sync.dma_start(out=sigma_bf[:], in_=sigma.partition_broadcast(P))
@@ -83,17 +89,28 @@ def tile_dmg_k_kernel(tc, batch_images, batch_labels, sigma, out):
                 nc.scalar.activation(out=whole, in_=whole, func=ACT.Exp, scale=minus_inv[:, 0:1])
 
                 folded = fold_pool.tile([P, pixels // 2, slots, PACK], F32)
-                nc.vector.tensor_tensor(
+                nc.gpsimd.tensor_tensor(
                     out=folded[:], in0=gauss[:, 0 : pixels // 2], in1=gauss[:, pixels // 2 : pixels], op=ALU.add
                 )
-                left = pixels // 4
-                while left >= 1:
-                    nc.vector.tensor_tensor(
+                left = pixels // 2
+                for fold in range(1, POOL_FOLDS):
+                    left //= 2
+                    nc.gpsimd.tensor_tensor(
                         out=folded[:, 0:left], in0=folded[:, 0:left], in1=folded[:, left : 2 * left], op=ALU.add
                     )
-                    left //= 2
-                recip = sum_pool.tile([P, slots, PACK], F32)
-                nc.vector.reciprocal(out=recip[:], in_=folded[:, 0])
+                sums = sum_pool.tile([P, slots * PACK], F32)
+                nc.vector.tensor_reduce(
+                    out=sums[:],
+                    in_=folded[:, 0:left].rearrange("p c s j -> p (s j) c"),
+                    axis=mybir.AxisListType.X,
+                    op=ALU.add,
+                )
+                recip_sb = sum_pool.tile([P, slots * PACK], F32)
+                nc.vector.reciprocal(out=recip_sb[:], in_=sums[:])
+                recip = recip_psum.tile([P, slots, PACK], F32)
+                nc.tensor.matmul(
+                    out=recip[:].rearrange("p s j -> p (s j)"), lhsT=ident[:], rhs=recip_sb[:], start=True, stop=True
+                )
 
                 grouped = norm_pool.tile([P, slots, pixels, PACK], BF16, align_bytes=64)
                 nc.vector.tensor_tensor(

@@ -18,7 +18,6 @@ XY = 2
 QUANT_WIDTH = 4096
 CHUNK_PASSES = 16
 STORE_IMAGES = 8
-POOL_FOLDS = 2
 
 IMAGES, LABELS, PIXELS = 64, 16384, 64
 FLOPS = 2 * IMAGES * LABELS * PIXELS * PIXELS
@@ -37,18 +36,18 @@ def tile_dmg_k_kernel(tc, batch_images, batch_labels, sigma, out):
     slots = XY * CHUNK_PASSES
     chunk_values = slots * pixels * PACK
     assert chunk_values % QUANT_WIDTH == 0
+    assert slots * PACK == P
 
     with ExitStack() as ctx:
         const = ctx.enter_context(tc.tile_pool(name="const", bufs=1))
         label_pool = ctx.enter_context(tc.tile_pool(name="labels", bufs=3))
         gauss_pool = ctx.enter_context(tc.tile_pool(name="gauss", bufs=3))
-        fold_pool = ctx.enter_context(tc.tile_pool(name="fold", bufs=2))
         sum_pool = ctx.enter_context(tc.tile_pool(name="sums", bufs=3))
         norm_pool = ctx.enter_context(tc.tile_pool(name="norm", bufs=2))
         mx_pool = ctx.enter_context(tc.tile_pool(name="mx", bufs=3))
         map_pool = ctx.enter_context(tc.tile_pool(name="maps", bufs=2))
         psum = ctx.enter_context(tc.psum_pool(name="psum", bufs=2))
-        recip_psum = ctx.enter_context(tc.psum_pool(name="recip_psum", bufs=2))
+        small_psum = ctx.enter_context(tc.psum_pool(name="small_psum", bufs=2))
 
         ident = const.tile([P, P], F32)
         make_identity(nc, ident[:])
@@ -88,29 +87,22 @@ def tile_dmg_k_kernel(tc, batch_images, batch_labels, sigma, out):
                 whole = gauss[:].rearrange("p c s j -> p (c s j)")
                 nc.scalar.activation(out=whole, in_=whole, func=ACT.Exp, scale=minus_inv[:, 0:1])
 
-                folded = fold_pool.tile([P, pixels // 2, slots, PACK], F32)
-                nc.gpsimd.tensor_tensor(
-                    out=folded[:], in0=gauss[:, 0 : pixels // 2], in1=gauss[:, pixels // 2 : pixels], op=ALU.add
-                )
-                left = pixels // 2
-                for fold in range(1, POOL_FOLDS):
-                    left //= 2
-                    nc.gpsimd.tensor_tensor(
-                        out=folded[:, 0:left], in0=folded[:, 0:left], in1=folded[:, left : 2 * left], op=ALU.add
+                sums_t = small_psum.tile([P, P], F32)
+                for c in range(pixels):
+                    nc.tensor.matmul(
+                        out=sums_t[:],
+                        lhsT=gauss[:, c].rearrange("p s j -> p (s j)"),
+                        rhs=ident[:],
+                        is_transpose=True,
+                        start=(c == 0),
+                        stop=(c == pixels - 1),
                     )
-                sums = sum_pool.tile([P, slots * PACK], F32)
-                nc.vector.tensor_reduce(
-                    out=sums[:],
-                    in_=folded[:, 0:left].rearrange("p c s j -> p (s j) c"),
-                    axis=mybir.AxisListType.X,
-                    op=ALU.add,
-                )
-                recip_sb = sum_pool.tile([P, slots * PACK], F32)
-                nc.vector.reciprocal(out=recip_sb[:], in_=sums[:])
-                recip = recip_psum.tile([P, slots, PACK], F32)
-                nc.tensor.matmul(
-                    out=recip[:].rearrange("p s j -> p (s j)"), lhsT=ident[:], rhs=recip_sb[:], start=True, stop=True
-                )
+                recip_t = sum_pool.tile([P, P], F32)
+                nc.vector.reciprocal(out=recip_t[:], in_=sums_t[:])
+                recip_ps = small_psum.tile([P, slots, PACK], F32)
+                nc.tensor.transpose(recip_ps[:].rearrange("p s j -> p (s j)"), recip_t[:], ident[:])
+                recip = sum_pool.tile([P, slots, PACK], F32)
+                nc.vector.tensor_copy(out=recip[:], in_=recip_ps[:])
 
                 grouped = norm_pool.tile([P, slots, pixels, PACK], BF16, align_bytes=64)
                 nc.vector.tensor_tensor(

@@ -5,6 +5,7 @@ from concourse.masks import make_identity
 
 F32 = mybir.dt.float32
 BF16 = mybir.dt.bfloat16
+I32 = mybir.dt.int32
 U32 = mybir.dt.uint32
 U8 = mybir.dt.uint8
 FP8X4 = mybir.dt.float8_e4m3fn_x4
@@ -18,6 +19,7 @@ XY = 2
 QUANT_WIDTH = 4096
 CHUNK_PASSES = 16
 STORE_IMAGES = 8
+VECTOR_COLUMNS = 16
 
 IMAGES, LABELS, PIXELS = 64, 16384, 64
 FLOPS = 2 * IMAGES * LABELS * PIXELS * PIXELS
@@ -30,30 +32,42 @@ def tile_dmg_k_kernel(tc, batch_images, batch_labels, sigma, out):
     height, width = out.shape[2], out.shape[3]
     assert height == width and XY * width == P
     pixels = width
+    scalar_columns = pixels - VECTOR_COLUMNS
     passes = labels // K_PASS
     assert labels % K_PASS == 0 and passes % CHUNK_PASSES == 0 and images % STORE_IMAGES == 0
-    chunks = passes // CHUNK_PASSES
+    chunks_of_image = passes // CHUNK_PASSES
+    chunks = images * chunks_of_image
     slots = XY * CHUNK_PASSES
+    assert slots * PACK == P
     chunk_values = slots * pixels * PACK
     assert chunk_values % QUANT_WIDTH == 0
-    assert slots * PACK == P
 
     with ExitStack() as ctx:
         const = ctx.enter_context(tc.tile_pool(name="const", bufs=1))
-        label_pool = ctx.enter_context(tc.tile_pool(name="labels", bufs=3))
         gauss_pool = ctx.enter_context(tc.tile_pool(name="gauss", bufs=3))
-        sum_pool = ctx.enter_context(tc.tile_pool(name="sums", bufs=3))
+        recip_pool = ctx.enter_context(tc.tile_pool(name="recip", bufs=2))
         norm_pool = ctx.enter_context(tc.tile_pool(name="norm", bufs=2))
-        mx_pool = ctx.enter_context(tc.tile_pool(name="mx", bufs=3))
+        mx_pool = ctx.enter_context(tc.tile_pool(name="mx", bufs=2))
         map_pool = ctx.enter_context(tc.tile_pool(name="maps", bufs=2))
-        psum = ctx.enter_context(tc.psum_pool(name="psum", bufs=2))
-        small_psum = ctx.enter_context(tc.psum_pool(name="small_psum", bufs=2))
+        map_psum = ctx.enter_context(tc.psum_pool(name="map_psum", bufs=2))
+        sum_psum = ctx.enter_context(tc.psum_pool(name="sum_psum", bufs=2))
+
+        lab = const.tile([P, images, passes, PACK * XY], BF16)
+        for b in range(images):
+            nc.sync.dma_start(
+                out=lab[:, b], in_=batch_labels[b].rearrange("(g p j) t -> p g (j t)", p=P, j=PACK)
+            )
 
         ident = const.tile([P, P], F32)
         make_identity(nc, ident[:])
 
+        column_i = const.tile([P, pixels], I32)
+        nc.gpsimd.iota(out=column_i[:], pattern=[[1, pixels]], base=0, channel_multiplier=0)
+        column = const.tile([P, pixels], F32)
+        nc.vector.tensor_copy(out=column[:], in_=column_i[:])
+
         sigma_bf = const.tile([P, 1], BF16)
-        nc.sync.dma_start(out=sigma_bf[:], in_=sigma.partition_broadcast(P))
+        nc.scalar.dma_start(out=sigma_bf[:], in_=sigma.partition_broadcast(P))
         sigma_f = const.tile([P, 1], F32)
         nc.vector.tensor_copy(out=sigma_f[:], in_=sigma_bf[:])
         minus_two_var = const.tile([P, 1], F32)
@@ -63,81 +77,131 @@ def tile_dmg_k_kernel(tc, batch_images, batch_labels, sigma, out):
         minus_inv = const.tile([P, 1], F32)
         nc.vector.reciprocal(out=minus_inv[:], in_=minus_two_var[:])
 
-        for b in range(images):
-            lab = label_pool.tile([P, passes, PACK * XY], BF16)
-            nc.sync.dma_start(
-                out=lab[:], in_=batch_labels[b].rearrange("(g p j) t -> p g (j t)", p=P, j=PACK)
-            )
-            if b % STORE_IMAGES == 0:
-                maps = map_pool.tile([P, STORE_IMAGES, pixels], F32)
-            acc = psum.tile([P, P], F32)
+        gauss_of, sums_t_of, recip_t_of, recip_ps_of, recip_of = {}, {}, {}, {}, {}
+        grouped_of, codes_of, scales_of, acc_of, maps_of = {}, {}, {}, {}, {}
 
-            for k in range(chunks):
-                chunk_lab = lab[:, k * CHUNK_PASSES : (k + 1) * CHUNK_PASSES, :].rearrange(
-                    "p g (j t) -> p g t j", t=XY
-                )
-                gauss = gauss_pool.tile([P, pixels, slots, PACK], F32)
-                for c in range(pixels):
-                    nc.scalar.activation(
-                        out=gauss[:, c].rearrange("p (g t) j -> p g t j", t=XY),
-                        in_=chunk_lab,
-                        func=ACT.Square,
-                        bias=float(-c),
-                    )
-                whole = gauss[:].rearrange("p c s j -> p (c s j)")
-                nc.scalar.activation(out=whole, in_=whole, func=ACT.Exp, scale=minus_inv[:, 0:1])
-
-                sums_t = small_psum.tile([P, P], F32)
-                for c in range(pixels):
-                    nc.tensor.matmul(
-                        out=sums_t[:],
-                        lhsT=gauss[:, c].rearrange("p s j -> p (s j)"),
-                        rhs=ident[:],
-                        is_transpose=True,
-                        start=(c == 0),
-                        stop=(c == pixels - 1),
-                    )
-                recip_t = sum_pool.tile([P, P], F32)
-                nc.vector.reciprocal(out=recip_t[:], in_=sums_t[:])
-                recip_ps = small_psum.tile([P, slots, PACK], F32)
-                nc.tensor.transpose(recip_ps[:].rearrange("p s j -> p (s j)"), recip_t[:], ident[:])
-                recip = sum_pool.tile([P, slots, PACK], F32)
-                nc.vector.tensor_copy(out=recip[:], in_=recip_ps[:])
-
-                grouped = norm_pool.tile([P, slots, pixels, PACK], BF16, align_bytes=64)
+        def exponentials(k):
+            first_pass = (k % chunks_of_image) * CHUNK_PASSES
+            chunk_lab = lab[:, k // chunks_of_image, first_pass : first_pass + CHUNK_PASSES, :]
+            gauss = gauss_pool.tile([P, pixels, slots, PACK], F32)
+            gauss_of[k] = gauss
+            rest = gauss[:, scalar_columns:pixels]
+            shape = [P, VECTOR_COLUMNS, CHUNK_PASSES, PACK]
+            for t in range(XY):
                 nc.vector.tensor_tensor(
-                    out=grouped[:],
-                    in0=gauss[:].rearrange("p c s j -> p s c j"),
-                    in1=recip[:].unsqueeze(2).to_broadcast([P, slots, pixels, PACK]),
-                    op=ALU.mult,
+                    out=rest.rearrange("p c (g t) j -> p t c g j", t=XY)[:, t],
+                    in0=chunk_lab.rearrange("p g (j t) -> p t g j", t=XY)[:, t].unsqueeze(1).to_broadcast(shape),
+                    in1=column[:, scalar_columns:pixels].unsqueeze(2).unsqueeze(3).to_broadcast(shape),
+                    op=ALU.subtract,
+                )
+            flat_rest = rest.rearrange("p c s j -> p (c s j)")
+            nc.vector.tensor_tensor(out=flat_rest, in0=flat_rest, in1=flat_rest, op=ALU.mult)
+            for c in range(scalar_columns):
+                nc.scalar.activation(
+                    out=gauss[:, c].rearrange("p (g t) j -> p g t j", t=XY),
+                    in_=chunk_lab.rearrange("p g (j t) -> p g t j", t=XY),
+                    func=ACT.Square,
+                    bias=float(-c),
+                )
+            whole = gauss[:].rearrange("p c s j -> p (c s j)")
+            nc.scalar.activation(out=whole, in_=whole, func=ACT.Exp, scale=minus_inv[:, 0:1])
+
+        def sum_over_pixels(k):
+            sums_t = sum_psum.tile([P, P], F32)
+            sums_t_of[k] = sums_t
+            for c in range(pixels):
+                nc.tensor.matmul(
+                    out=sums_t[:],
+                    lhsT=gauss_of[k][:, c].rearrange("p s j -> p (s j)"),
+                    rhs=ident[:],
+                    is_transpose=True,
+                    start=(c == 0),
+                    stop=(c == pixels - 1),
                 )
 
-                codes = mx_pool.tile([P, slots * pixels], U32, align_bytes=64)
-                scales = mx_pool.tile([P, slots * pixels], U8, align_bytes=64)
-                flat = grouped[:].rearrange("p s c j -> p (s c j)")
-                for q in range(chunk_values // QUANT_WIDTH):
-                    words = slice(q * QUANT_WIDTH // PACK, (q + 1) * QUANT_WIDTH // PACK)
-                    nc.vector.quantize_mx(
-                        out=codes[:, words].bitcast(FP8X4),
-                        scales=scales[:, words],
-                        in_=flat[:, q * QUANT_WIDTH : (q + 1) * QUANT_WIDTH],
-                    )
+        def reciprocal_of_sums(k):
+            recip_t = recip_pool.tile([P, P], F32)
+            recip_t_of[k] = recip_t
+            nc.vector.reciprocal(out=recip_t[:], in_=sums_t_of[k][:])
 
-                for g in range(CHUNK_PASSES):
-                    cols = slice(g * P, (g + 1) * P)
-                    nc.tensor.matmul_mx(
-                        out=acc[:],
-                        lhsT=codes[:, cols].bitcast(FP8X4),
-                        lhsT_scale=scales[:, cols],
-                        rhs=codes[:, cols].bitcast(FP8X4),
-                        rhs_scale=scales[:, cols],
-                        start=(k == 0 and g == 0),
-                        stop=(k == chunks - 1 and g == CHUNK_PASSES - 1),
-                    )
+        def transpose_back(k):
+            recip_ps = sum_psum.tile([P, slots, PACK], F32)
+            recip_ps_of[k] = recip_ps
+            nc.tensor.transpose(recip_ps[:].rearrange("p s j -> p (s j)"), recip_t_of[k][:], ident[:])
 
-            nc.scalar.copy(out=maps[pixels:P, b % STORE_IMAGES, :], in_=acc[pixels:P, 0:pixels])
-            if b % STORE_IMAGES == STORE_IMAGES - 1:
-                first = b - (STORE_IMAGES - 1)
-                nc.sync.dma_start(
-                    out=out[first : b + 1, 0].rearrange("b h w -> h b w"), in_=maps[pixels:P, :, :]
+        def keep_reciprocal(k):
+            recip = recip_pool.tile([P, slots, PACK], F32)
+            recip_of[k] = recip
+            nc.vector.tensor_copy(out=recip[:], in_=recip_ps_of[k][:])
+
+        def normalise(k):
+            grouped = norm_pool.tile([P, slots, pixels, PACK], BF16, align_bytes=64)
+            grouped_of[k] = grouped
+            nc.vector.tensor_tensor(
+                out=grouped[:],
+                in0=gauss_of[k][:].rearrange("p c s j -> p s c j"),
+                in1=recip_of[k][:].unsqueeze(2).to_broadcast([P, slots, pixels, PACK]),
+                op=ALU.mult,
+            )
+
+        def quantise(k):
+            codes = mx_pool.tile([P, slots * pixels], U32, align_bytes=64)
+            scales = mx_pool.tile([P, slots * pixels], U8, align_bytes=64)
+            codes_of[k], scales_of[k] = codes, scales
+            flat = grouped_of[k][:].rearrange("p s c j -> p (s c j)")
+            for q in range(chunk_values // QUANT_WIDTH):
+                words = slice(q * QUANT_WIDTH // PACK, (q + 1) * QUANT_WIDTH // PACK)
+                nc.vector.quantize_mx(
+                    out=codes[:, words].bitcast(FP8X4),
+                    scales=scales[:, words],
+                    in_=flat[:, q * QUANT_WIDTH : (q + 1) * QUANT_WIDTH],
                 )
+
+        def multiply(k):
+            b = k // chunks_of_image
+            first_chunk = k % chunks_of_image == 0
+            last_chunk = k % chunks_of_image == chunks_of_image - 1
+            if first_chunk:
+                acc = map_psum.tile([P, P], F32)
+                acc_of[b] = acc
+            codes, scales = codes_of[k], scales_of[k]
+            for g in range(CHUNK_PASSES):
+                cols = slice(g * P, (g + 1) * P)
+                nc.tensor.matmul_mx(
+                    out=acc_of[b][:],
+                    lhsT=codes[:, cols].bitcast(FP8X4),
+                    lhsT_scale=scales[:, cols],
+                    rhs=codes[:, cols].bitcast(FP8X4),
+                    rhs_scale=scales[:, cols],
+                    start=(first_chunk and g == 0),
+                    stop=(last_chunk and g == CHUNK_PASSES - 1),
+                )
+            if last_chunk:
+                group = b // STORE_IMAGES
+                if b % STORE_IMAGES == 0:
+                    maps = map_pool.tile([P, STORE_IMAGES, pixels], F32)
+                    maps_of[group] = maps
+                nc.scalar.copy(out=maps_of[group][pixels:P, b % STORE_IMAGES, :], in_=acc_of[b][pixels:P, 0:pixels])
+                if b % STORE_IMAGES == STORE_IMAGES - 1:
+                    nc.sync.dma_start(
+                        out=out[b - (STORE_IMAGES - 1) : b + 1, 0].rearrange("b h w -> h b w"),
+                        in_=maps_of[group][pixels:P, :, :],
+                    )
+
+        ctx.enter_context(tc.manual_schedule())
+        for i in range(-1, chunks + 2):
+            if i + 1 < chunks:
+                exponentials(i + 1)
+            if 0 <= i - 2:
+                multiply(i - 2)
+            if 0 <= i < chunks:
+                sum_over_pixels(i)
+            if 0 <= i - 1 < chunks:
+                normalise(i - 1)
+            if 0 <= i < chunks:
+                reciprocal_of_sums(i)
+                transpose_back(i)
+            if 0 <= i - 1 < chunks:
+                quantise(i - 1)
+            if 0 <= i < chunks:
+                keep_reciprocal(i)

@@ -77,7 +77,7 @@ def tile_dmg_k_kernel(tc, batch_images, batch_labels, sigma, out):
         minus_inv = const.tile([P, 1], F32)
         nc.vector.reciprocal(out=minus_inv[:], in_=minus_two_var[:])
 
-        gauss_of, sums_t_of, recip_t_of, recip_ps_of, recip_of = {}, {}, {}, {}, {}
+        gauss_of, sums_t_of, recip_t_of, recip_of = {}, {}, {}, {}
         grouped_of, codes_of, scales_of, acc_of, maps_of = {}, {}, {}, {}, {}
 
         def exponentials(k):
@@ -125,14 +125,9 @@ def tile_dmg_k_kernel(tc, batch_images, batch_labels, sigma, out):
             nc.vector.reciprocal(out=recip_t[:], in_=sums_t_of[k][:])
 
         def transpose_back(k):
-            recip_ps = sum_psum.tile([P, slots, PACK], F32)
-            recip_ps_of[k] = recip_ps
-            nc.tensor.transpose(recip_ps[:].rearrange("p s j -> p (s j)"), recip_t_of[k][:], ident[:])
-
-        def keep_reciprocal(k):
-            recip = recip_pool.tile([P, slots, PACK], F32)
+            recip = sum_psum.tile([P, slots, PACK], F32)
             recip_of[k] = recip
-            nc.vector.tensor_copy(out=recip[:], in_=recip_ps_of[k][:])
+            nc.tensor.transpose(recip[:].rearrange("p s j -> p (s j)"), recip_t_of[k][:], ident[:])
 
         def normalise(k):
             grouped = norm_pool.tile([P, slots, pixels, PACK], BF16, align_bytes=64)
@@ -203,5 +198,3 @@ def tile_dmg_k_kernel(tc, batch_images, batch_labels, sigma, out):
                 transpose_back(i)
             if 0 <= i - 1 < chunks:
                 quantise(i - 1)
-            if 0 <= i < chunks:
-                keep_reciprocal(i)

from contextlib import ExitStack

import concourse.mybir as mybir
from concourse.masks import make_identity

F32 = mybir.dt.float32
BF16 = mybir.dt.bfloat16
I32 = mybir.dt.int32
U32 = mybir.dt.uint32
U8 = mybir.dt.uint8
FP8X4 = mybir.dt.float8_e4m3fn_x4
ACT = mybir.ActivationFunctionType
ALU = mybir.AluOpType

P = 128
PACK = 4
K_PASS = P * PACK
XY = 2
QUANT_WIDTH = 4096
CHUNK_PASSES = 16
STORE_IMAGES = 8
VECTOR_COLUMNS = 16

IMAGES, LABELS, PIXELS = 64, 16384, 64
FLOPS = 2 * IMAGES * LABELS * PIXELS * PIXELS
BYTES = IMAGES * LABELS * XY * 2 + 2 + IMAGES * PIXELS * PIXELS * 4


def tile_dmg_k_kernel(tc, batch_images, batch_labels, sigma, out):
    nc = tc.nc
    images, labels = batch_labels.shape[0], batch_labels.shape[1]
    height, width = out.shape[2], out.shape[3]
    assert height == width and XY * width == P
    pixels = width
    scalar_columns = pixels - VECTOR_COLUMNS
    passes = labels // K_PASS
    assert labels % K_PASS == 0 and passes % CHUNK_PASSES == 0 and images % STORE_IMAGES == 0
    chunks_of_image = passes // CHUNK_PASSES
    chunks = images * chunks_of_image
    slots = XY * CHUNK_PASSES
    assert slots * PACK == P
    chunk_values = slots * pixels * PACK
    assert chunk_values % QUANT_WIDTH == 0

    with ExitStack() as ctx:
        const = ctx.enter_context(tc.tile_pool(name="const", bufs=1))
        gauss_pool = ctx.enter_context(tc.tile_pool(name="gauss", bufs=3))
        recip_pool = ctx.enter_context(tc.tile_pool(name="recip", bufs=2))
        norm_pool = ctx.enter_context(tc.tile_pool(name="norm", bufs=2))
        mx_pool = ctx.enter_context(tc.tile_pool(name="mx", bufs=2))
        map_pool = ctx.enter_context(tc.tile_pool(name="maps", bufs=2))
        map_psum = ctx.enter_context(tc.psum_pool(name="map_psum", bufs=2))
        sum_psum = ctx.enter_context(tc.psum_pool(name="sum_psum", bufs=2))

        lab = const.tile([P, images, passes, PACK * XY], BF16)
        for b in range(images):
            nc.sync.dma_start(
                out=lab[:, b], in_=batch_labels[b].rearrange("(g p j) t -> p g (j t)", p=P, j=PACK)
            )

        ident = const.tile([P, P], F32)
        make_identity(nc, ident[:])

        column_i = const.tile([P, pixels], I32)
        nc.gpsimd.iota(out=column_i[:], pattern=[[1, pixels]], base=0, channel_multiplier=0)
        column = const.tile([P, pixels], F32)
        nc.vector.tensor_copy(out=column[:], in_=column_i[:])

        sigma_bf = const.tile([P, 1], BF16)
        nc.scalar.dma_start(out=sigma_bf[:], in_=sigma.partition_broadcast(P))
        sigma_f = const.tile([P, 1], F32)
        nc.vector.tensor_copy(out=sigma_f[:], in_=sigma_bf[:])
        minus_two_var = const.tile([P, 1], F32)
        nc.vector.scalar_tensor_tensor(
            out=minus_two_var[:], in0=sigma_f[:], scalar=-2.0, in1=sigma_f[:], op0=ALU.mult, op1=ALU.mult
        )
        minus_inv = const.tile([P, 1], F32)
        nc.vector.reciprocal(out=minus_inv[:], in_=minus_two_var[:])

        gauss_of, sums_t_of, recip_t_of, recip_of = {}, {}, {}, {}
        grouped_of, codes_of, scales_of, acc_of, maps_of = {}, {}, {}, {}, {}

        def exponentials(k):
            first_pass = (k % chunks_of_image) * CHUNK_PASSES
            chunk_lab = lab[:, k // chunks_of_image, first_pass : first_pass + CHUNK_PASSES, :]
            gauss = gauss_pool.tile([P, pixels, slots, PACK], F32)
            gauss_of[k] = gauss
            rest = gauss[:, scalar_columns:pixels]
            shape = [P, VECTOR_COLUMNS, CHUNK_PASSES, PACK]
            for t in range(XY):
                nc.vector.tensor_tensor(
                    out=rest.rearrange("p c (g t) j -> p t c g j", t=XY)[:, t],
                    in0=chunk_lab.rearrange("p g (j t) -> p t g j", t=XY)[:, t].unsqueeze(1).to_broadcast(shape),
                    in1=column[:, scalar_columns:pixels].unsqueeze(2).unsqueeze(3).to_broadcast(shape),
                    op=ALU.subtract,
                )
            flat_rest = rest.rearrange("p c s j -> p (c s j)")
            nc.vector.tensor_tensor(out=flat_rest, in0=flat_rest, in1=flat_rest, op=ALU.mult)
            for c in range(scalar_columns):
                nc.scalar.activation(
                    out=gauss[:, c].rearrange("p (g t) j -> p g t j", t=XY),
                    in_=chunk_lab.rearrange("p g (j t) -> p g t j", t=XY),
                    func=ACT.Square,
                    bias=float(-c),
                )
            whole = gauss[:].rearrange("p c s j -> p (c s j)")
            nc.scalar.activation(out=whole, in_=whole, func=ACT.Exp, scale=minus_inv[:, 0:1])

        def sum_over_pixels(k):
            sums_t = sum_psum.tile([P, P], F32)
            sums_t_of[k] = sums_t
            for c in range(pixels):
                nc.tensor.matmul(
                    out=sums_t[:],
                    lhsT=gauss_of[k][:, c].rearrange("p s j -> p (s j)"),
                    rhs=ident[:],
                    is_transpose=True,
                    start=(c == 0),
                    stop=(c == pixels - 1),
                )

        def reciprocal_of_sums(k):
            recip_t = recip_pool.tile([P, P], F32)
            recip_t_of[k] = recip_t
            nc.vector.reciprocal(out=recip_t[:], in_=sums_t_of[k][:])

        def transpose_back(k):
            recip = sum_psum.tile([P, slots, PACK], F32)
            recip_of[k] = recip
            nc.tensor.transpose(recip[:].rearrange("p s j -> p (s j)"), recip_t_of[k][:], ident[:])

        def normalise(k):
            grouped = norm_pool.tile([P, slots, pixels, PACK], BF16, align_bytes=64)
            grouped_of[k] = grouped
            nc.vector.tensor_tensor(
                out=grouped[:],
                in0=gauss_of[k][:].rearrange("p c s j -> p s c j"),
                in1=recip_of[k][:].unsqueeze(2).to_broadcast([P, slots, pixels, PACK]),
                op=ALU.mult,
            )

        def quantise(k):
            codes = mx_pool.tile([P, slots * pixels], U32, align_bytes=64)
            scales = mx_pool.tile([P, slots * pixels], U8, align_bytes=64)
            codes_of[k], scales_of[k] = codes, scales
            flat = grouped_of[k][:].rearrange("p s c j -> p (s c j)")
            for q in range(chunk_values // QUANT_WIDTH):
                words = slice(q * QUANT_WIDTH // PACK, (q + 1) * QUANT_WIDTH // PACK)
                nc.vector.quantize_mx(
                    out=codes[:, words].bitcast(FP8X4),
                    scales=scales[:, words],
                    in_=flat[:, q * QUANT_WIDTH : (q + 1) * QUANT_WIDTH],
                )

        def multiply(k):
            b = k // chunks_of_image
            first_chunk = k % chunks_of_image == 0
            last_chunk = k % chunks_of_image == chunks_of_image - 1
            if first_chunk:
                acc = map_psum.tile([P, P], F32)
                acc_of[b] = acc
            codes, scales = codes_of[k], scales_of[k]
            for g in range(CHUNK_PASSES):
                cols = slice(g * P, (g + 1) * P)
                nc.tensor.matmul_mx(
                    out=acc_of[b][:],
                    lhsT=codes[:, cols].bitcast(FP8X4),
                    lhsT_scale=scales[:, cols],
                    rhs=codes[:, cols].bitcast(FP8X4),
                    rhs_scale=scales[:, cols],
                    start=(first_chunk and g == 0),
                    stop=(last_chunk and g == CHUNK_PASSES - 1),
                )
            if last_chunk:
                group = b // STORE_IMAGES
                if b % STORE_IMAGES == 0:
                    maps = map_pool.tile([P, STORE_IMAGES, pixels], F32)
                    maps_of[group] = maps
                nc.scalar.copy(out=maps_of[group][pixels:P, b % STORE_IMAGES, :], in_=acc_of[b][pixels:P, 0:pixels])
                if b % STORE_IMAGES == STORE_IMAGES - 1:
                    nc.sync.dma_start(
                        out=out[b - (STORE_IMAGES - 1) : b + 1, 0].rearrange("b h w -> h b w"),
                        in_=maps_of[group][pixels:P, :, :],
                    )

        ctx.enter_context(tc.manual_schedule())
        for i in range(-1, chunks + 2):
            if i + 1 < chunks:
                exponentials(i + 1)
            if 0 <= i - 2:
                multiply(i - 2)
            if 0 <= i < chunks:
                sum_over_pixels(i)
            if 0 <= i - 1 < chunks:
                normalise(i - 1)
            if 0 <= i < chunks:
                reciprocal_of_sums(i)
                transpose_back(i)
            if 0 <= i - 1 < chunks:
                quantise(i - 1)
